import numpy as np
import ml_dtypes


def mxq(x, axis, fmt="e4m3"):
    dtype, down = {"e4m3": (ml_dtypes.float8_e4m3fn, 7), "e5m2": (ml_dtypes.float8_e5m2, 14)}[fmt]
    v = np.moveaxis(np.asarray(x, np.float32).astype(ml_dtypes.bfloat16).astype(np.float64), axis, -1)
    blocks = v.reshape(v.shape[:-1] + (-1, 32))
    amax = np.abs(blocks).max(-1, keepdims=True)
    byte = np.maximum(np.where(amax > 0, np.frexp(amax)[1] - 1 + 127, 0) - down, 1)
    scale = np.exp2(byte - 127.0)
    codes = (blocks / scale).astype(np.float32).astype(dtype).astype(np.float64)
    return np.moveaxis((codes * scale).reshape(v.shape), -1, axis)


WIDE = False


def mx_kscale(k):
    if not WIDE:
        return np.ones(k)
    levels = np.array([10, -10, 5, -5, 0])
    a = np.random.permutation(np.resize(levels, k // 512 * 4)).reshape(k // 512, 4)
    idx = np.arange(k)
    return np.exp2(a[idx // 512, idx % 128 // 32])


BF16 = ml_dtypes.bfloat16


def bf(x):
    return np.asarray(x, np.float32).astype(BF16)


def f64(x):
    return np.asarray(x).astype(np.float64)


B, T, D, H = 8, 512, 1024, 384


def sigmoid(v):
    return 1.0 / (1.0 + np.exp(-v))


def setup_inputs():
    s = mx_kscale(D)
    return {"x": bf(np.random.standard_normal((B, T, D)) * s),
            "Wq": bf(np.random.standard_normal((H, D)) * 1.0 / np.sqrt(D) / s),
            "bq": bf(np.random.standard_normal(H) * 0.5),
            "Wk": bf(np.random.standard_normal((H, D)) * 0.6 / np.sqrt(D) / s),
            "bk": bf(np.random.standard_normal(H) * 0.3),
            "Wv": bf(np.random.standard_normal((H, D)) * 2.0 / np.sqrt(D) / s),
            "bv": bf(np.random.standard_normal(H) * 0.5),
            "wbias": bf(np.random.uniform(0.0, 1.0, H))}


def reference(x, Wq, bq, Wk, bk, Wv, bv, wbias):
    xq = mxq(f64(x), 2, "e4m3")
    Q = (xq @ mxq(f64(Wq), 1, "e4m3").T) + f64(bq)
    K = (xq @ mxq(f64(Wk), 1, "e4m3").T) + f64(bk)
    V = (xq @ mxq(f64(Wv), 1, "e4m3").T) + f64(bv)
    Q_sig = sigmoid(Q)
    numer = np.exp(K + f64(wbias))
    denom = numer.sum(axis=0)
    weighted = (numer * V).sum(axis=0) / denom
    Yt = Q_sig * weighted
    return Yt

@@ -1,0 +1,255 @@
+from contextlib import ExitStack
+
+import concourse.masks as masks
+import concourse.mybir as mybir
+
+F32 = mybir.dt.float32
+BF16 = mybir.dt.bfloat16
+U32 = mybir.dt.uint32
+U8 = mybir.dt.uint8
+FP8X4 = mybir.dt.float8_e4m3fn_x4
+ACT = mybir.ActivationFunctionType
+ALU = mybir.AluOpType
+
+B, T, DM, H = 8, 512, 1024, 384
+P = 128
+J = T // P
+NPAIR = B * J // 2
+FLOPS = 2 * B * T * DM * 3 * H
+
+PIN = True
+LOOK = 2
+ZL = 10
+G_SUM_E = True
+G_P7_MOD = 2
+XBUFS = 5
+
+
+def tile_aftattention_t_kernel(tc, x, Wq, bq, Wk, bk, Wv, bv, wbias, out):
+    nc = tc.nc
+    with ExitStack() as ctx:
+        keep = ctx.enter_context(tc.tile_pool(name="keep", bufs=1))
+        stage = ctx.enter_context(tc.tile_pool(name="stage", bufs=3))
+        psum = ctx.enter_context(tc.psum_pool(name="psum", bufs=1))
+        if PIN:
+            ctx.enter_context(tc.manual_schedule())
+
+        nbufs = {"kk": 3, "vv": 3, "tp": 2}
+
+        def bank(tag):
+            return psum.tile([P, 512], F32, name="bank_" + tag, tag=tag, bufs=nbufs[tag])
+
+        ident = keep.tile([P, P], F32, name="ident")
+        masks.make_identity(nc, ident[:])
+
+        w_raw = keep.tile([P, 9, DM], BF16, name="w_raw")
+        w_grp = keep.tile([P, 3 * 2 * H * 4], BF16, name="w_grp", align_bytes=64)
+        w_codes = keep.tile([P, 3, 2, H], U32, name="w_codes", align_bytes=64)
+        w_sc = keep.tile([P, 3, 2, H], U8, name="w_sc", align_bytes=64)
+        x_codes = keep.tile([P, B, 2, J * P], U32, name="x_codes", align_bytes=64)
+        x_sc = keep.tile([P, B, 2, J * P], U8, name="x_sc", align_bytes=64)
+        d_sum = keep.tile([P, J, H], F32, name="d_sum")
+        n_sum = keep.tile([P, J, H], F32, name="n_sum")
+        r_d = keep.tile([P, J, H], F32, name="r_d")
+        bq_b = keep.tile([P, H], BF16, name="bq_b")
+        bv_b = keep.tile([P, H], BF16, name="bv_b")
+
+        w_dram = (Wk, Wv, Wq)
+        x_tiles = {}
+        grp_tiles = {}
+
+        def load_w(m, r):
+            nc.sync.dma_start(out=w_raw[:, 3 * m + r, :], in_=w_dram[m][r * P : (r + 1) * P, :])
+
+        def load_x(b, halves):
+            xr = stage.tile([P, J, DM], BF16, name="x_raw", tag="x_raw", bufs=XBUFS)
+            x_tiles[b] = xr
+            src = x[b].rearrange("(p j) k -> p j k", j=J)
+            if halves:
+                nc.sync.dma_start(out=xr[:, 0:2, :], in_=src[:, 0:2, :])
+            else:
+                nc.sync.dma_start(out=xr[:], in_=src)
+
+        def load_x_second_half(b):
+            src = x[b].rearrange("(p j) k -> p j k", j=J)
+            nc.sync.dma_start(out=x_tiles[b][:, 2:4, :], in_=src[:, 2:4, :])
+
+        def transpose_words(dst_bank, src_bf16):
+            words = src_bf16.bitcast(F32)
+            for c in range(4):
+                nc.tensor.transpose(
+                    dst_bank[:, c * P : (c + 1) * P], words[:, c * P : (c + 1) * P], ident[:]
+                )
+
+        w_grp32 = w_grp[:].bitcast(F32).rearrange("p (m g h u) -> p m g h u", m=3, g=2, u=2)
+
+        def t_w(m, r, tag, on_scalar):
+            bk_ = bank(tag)
+            transpose_words(bk_, w_raw[:, 3 * m + r, :])
+            src = bk_[:].rearrange("p (g u r) -> p g r u", g=2, u=2)
+            dst = w_grp32[:, m, :, r * P : (r + 1) * P, :]
+            if on_scalar:
+                nc.scalar.copy(out=dst, in_=src)
+            else:
+                nc.vector.tensor_copy(out=dst, in_=src)
+
+        def q_w(m, c0, c1):
+            for g in range(2):
+                off = ((m * 2 + g) * H + c0) * 4
+                nc.vector.quantize_mx(
+                    out=w_codes[:, m, g, c0:c1].bitcast(FP8X4),
+                    scales=w_sc[:, m, g, c0:c1],
+                    in_=w_grp[:, off : off + 4 * (c1 - c0)],
+                )
+
+        def t_x(q):
+            b, half = q // 2, q % 2
+            grp = stage.tile([P, 2048], BF16, name="x_grp", tag="x_grp", bufs=3, align_bytes=64)
+            grp_tiles[q] = grp
+            grp32 = grp[:].bitcast(F32).rearrange("p (g r u) -> p g r u", g=2, u=2)
+            for s in range(2):
+                bk_ = bank("tp")
+                transpose_words(bk_, x_tiles[b][:, 2 * half + s, :])
+                nc.scalar.copy(
+                    out=grp32[:, :, s * P : (s + 1) * P, :],
+                    in_=bk_[:].rearrange("p (g u r) -> p g r u", g=2, u=2),
+                )
+            if half == 1 and b + XBUFS < B:
+                load_x(b + XBUFS, False)
+
+        def q_x(q):
+            b, half = q // 2, q % 2
+            grp = grp_tiles[q]
+            for g in range(2):
+                nc.vector.quantize_mx(
+                    out=x_codes[:, b, g, half * 256 : (half + 1) * 256].bitcast(FP8X4),
+                    scales=x_sc[:, b, g, half * 256 : (half + 1) * 256],
+                    in_=grp[:, g * 1024 : (g + 1) * 1024],
+                )
+
+        def project(dst_bank, b, j, m):
+            for c0, c1 in ((0, 256), (256, H)):
+                for g in range(2):
+                    nc.tensor.matmul_mx(
+                        out=dst_bank[:, c0:c1],
+                        lhsT=x_codes[:, b, g, j * P : (j + 1) * P].bitcast(FP8X4),
+                        lhsT_scale=x_sc[:, b, g, j * P : (j + 1) * P],
+                        rhs=w_codes[:, m, g, c0:c1].bitcast(FP8X4),
+                        rhs_scale=w_sc[:, m, g, c0:c1],
+                        start=(g == 0),
+                        stop=(g == 1),
+                    )
+
+        def kv_pair(q, mid):
+            b, half = q // 2, q % 2
+            js = slice(2 * half, 2 * half + 2)
+            if b > 0:
+                e_t = stage.tile([P, 2, H], F32, name="e_t", tag="e_t", bufs=3)
+                p_t = stage.tile([P, 2, H], F32, name="p_t", tag="p_t", bufs=3)
+            for s in range(2):
+                j = 2 * half + s
+                kb = bank("kk")
+                project(kb, b, j, 0)
+                vb = bank("vv")
+                project(vb, b, j, 1)
+                e_dst = d_sum[:, j, :] if b == 0 else e_t[:, s, :]
+                p_dst = n_sum[:, j, :] if b == 0 else p_t[:, s, :]
+                nc.scalar.activation(out=e_dst, in_=kb[:, 0:H], func=ACT.Exp)
+                nc.vector.tensor_tensor(out=p_dst, in0=vb[:, 0:H], in1=e_dst, op=ALU.mult)
+                if s == 0 and mid:
+                    q_w(2, 256, H)
+            if b > 0:
+                nc.vector.tensor_tensor(out=n_sum[:, js, :], in0=n_sum[:, js, :], in1=p_t[:], op=ALU.add)
+                eng = nc.gpsimd if G_SUM_E else nc.vector
+                eng.tensor_tensor(out=d_sum[:, js, :], in0=d_sum[:, js, :], in1=e_t[:], op=ALU.add)
+
+        for r in range(3):
+            load_w(0, r)
+        load_x(0, True)
+        for r in range(3):
+            load_w(1, r)
+        load_x_second_half(0)
+        load_x(1, True)
+        load_x_second_half(1)
+        load_x(2, False)
+        nc.sync.dma_start(out=w_raw[:, 6:9, :], in_=Wq.rearrange("(r p) k -> p r k", p=P))
+        load_x(3, False)
+        load_x(4, False)
+        nc.sync.dma_start(out=bq_b[:], in_=bq.partition_broadcast(P))
+        nc.sync.dma_start(out=bv_b[:], in_=bv.partition_broadcast(P))
+
+        for r in range(3):
+            t_w(0, r, "kk", r % 2 == 0)
+        t_x(0)
+        q_w(0, 0, 256)
+        q_w(0, 256, H)
+        for r in range(3):
+            t_w(1, r, "vv", r % 2 == 0)
+        t_x(1)
+        q_x(0)
+        q_w(1, 0, 256)
+        q_w(1, 256, H)
+
+        for q in range(NPAIR):
+            if q + LOOK < NPAIR:
+                t_x(q + LOOK)
+            elif q + LOOK == NPAIR:
+                t_w(2, 0, "tp", True)
+                t_w(2, 1, "tp", True)
+            else:
+                t_w(2, 2, "tp", True)
+            if q + 1 < NPAIR:
+                q_x(q + 1)
+            else:
+                q_w(2, 0, 256)
+            kv_pair(q, q == NPAIR - 1)
+
+        tags = ("kk", "vv", "kk", "vv", "kk", "vv", "tp", "tp")
+        zq_tiles = {}
+        o_tiles = {}
+
+        def q_front(t):
+            b, j = t // J, t % J
+            qb = bank(tags[t % 8])
+            project(qb, b, j, 2)
+            zq = stage.tile([P, H], F32, name="zq", tag="zq", bufs=ZL + 2)
+            zq_tiles[t] = zq
+            nc.vector.tensor_tensor(out=zq[:], in0=qb[:, 0:H], in1=bq_b[:], op=ALU.add)
+
+        def q_back(t):
+            b, j = t // J, t % J
+            if j == 0:
+                o_tiles[b] = stage.tile([P, J, H], F32, name="o_sb", tag="o_sb", bufs=3)
+            o_sb = o_tiles[b]
+            sg = stage.tile([P, H], F32, name="sg", tag="sg", bufs=4)
+            nc.scalar.activation(out=sg[:], in_=zq_tiles[t][:], func=ACT.Sigmoid)
+            eng = nc.gpsimd if (G_P7_MOD and t % G_P7_MOD == 1) else nc.vector
+            eng.tensor_tensor(out=o_sb[:, j, :], in0=sg[:], in1=n_sum[:, j, :], op=ALU.mult)
+            dst = out[b].rearrange("(p j) h -> p j h", j=J)
+            if b == B - 1:
+                if j % 2 == 1:
+                    nc.sync.dma_start(out=dst[:, j - 1 : j + 1, :], in_=o_sb[:, j - 1 : j + 1, :])
+            elif j == J - 1:
+                nc.sync.dma_start(out=dst, in_=o_sb[:])
+
+        for t in range(ZL):
+            q_front(t)
+        for hp in range(2):
+            js = slice(2 * hp, 2 * hp + 2)
+            nc.scalar.activation(out=r_d[:, js, :], in_=d_sum[:, js, :], func=ACT.Ln)
+        for hp in range(2):
+            js = slice(2 * hp, 2 * hp + 2)
+            nc.scalar.activation(out=r_d[:, js, :], in_=r_d[:, js, :], func=ACT.Exp, scale=-1.0)
+        for hp in range(2):
+            js = slice(2 * hp, 2 * hp + 2)
+            nc.vector.tensor_tensor(out=n_sum[:, js, :], in0=n_sum[:, js, :], in1=r_d[:, js, :], op=ALU.mult)
+            nc.vector.tensor_tensor(
+                out=n_sum[:, js, :],
+                in0=n_sum[:, js, :],
+                in1=bv_b[:].unsqueeze(1).to_broadcast([P, 2, H]),
+                op=ALU.add,
+            )
+        for t in range(B * J):
+            q_back(t)
+            if t + ZL < B * J:
+                q_front(t + ZL)

@@ -20,8 +20,8 @@ FLOPS = 2 * B * T * DM * 3 * H
 PIN = True
 LOOK = 2
 ZL = 10
-G_SUM_E = True
-G_P7_MOD = 2
+G_SUM_E = False
+G_P7_MOD = 0
 XBUFS = 5
 
 

@@ -14,65 +14,70 @@ ALU = mybir.AluOpType
 B, T, DM, H = 8, 512, 1024, 384
 P = 128
 J = T // P
-NPAIR = B * J // 2
+HB = H // P
 FLOPS = 2 * B * T * DM * 3 * H
 
 PIN = True
-LOOK = 2
-ZL = 10
-G_SUM_E = False
-G_P7_MOD = 0
-XBUFS = 5
+LASTK = 3
+DV = LASTK - 1
+QP1 = (0, 1, 1, 1, 1)
+QP2 = (2, 2, 3)
+QP3 = 4
+PRE = 2
+QEVERY = 3
+XTRA0 = 1
+AHEAD = 5
+OBUFS = 3
+XBUFS = 4
+MK, MV, MQ = 0, 1, 2
 
 
 def tile_aftattention_t_kernel(tc, x, Wq, bq, Wk, bk, Wv, bv, wbias, out):
     nc = tc.nc
     with ExitStack() as ctx:
         keep = ctx.enter_context(tc.tile_pool(name="keep", bufs=1))
-        stage = ctx.enter_context(tc.tile_pool(name="stage", bufs=3))
-        psum = ctx.enter_context(tc.psum_pool(name="psum", bufs=1))
+        stage = ctx.enter_context(tc.tile_pool(name="stage", bufs=2))
+        psum = ctx.enter_context(tc.psum_pool(name="psum", bufs=8))
         if PIN:
             ctx.enter_context(tc.manual_schedule())
 
-        nbufs = {"kk": 3, "vv": 3, "tp": 2}
-
-        def bank(tag):
-            return psum.tile([P, 512], F32, name="bank_" + tag, tag=tag, bufs=nbufs[tag])
+        def bank():
+            return psum.tile([P, 512], F32, name="ps", tag="ps", bufs=8)
 
         ident = keep.tile([P, P], F32, name="ident")
         masks.make_identity(nc, ident[:])
 
-        w_raw = keep.tile([P, 9, DM], BF16, name="w_raw")
-        w_grp = keep.tile([P, 3 * 2 * H * 4], BF16, name="w_grp", align_bytes=64)
-        w_codes = keep.tile([P, 3, 2, H], U32, name="w_codes", align_bytes=64)
-        w_sc = keep.tile([P, 3, 2, H], U8, name="w_sc", align_bytes=64)
-        x_codes = keep.tile([P, B, 2, J * P], U32, name="x_codes", align_bytes=64)
-        x_sc = keep.tile([P, B, 2, J * P], U8, name="x_sc", align_bytes=64)
-        d_sum = keep.tile([P, J, H], F32, name="d_sum")
-        n_sum = keep.tile([P, J, H], F32, name="n_sum")
-        r_d = keep.tile([P, J, H], F32, name="r_d")
-        bq_b = keep.tile([P, H], BF16, name="bq_b")
-        bv_b = keep.tile([P, H], BF16, name="bv_b")
+        w_codes = keep.tile([P, 3, 2 * H], U32, name="w_codes", align_bytes=64)
+        w_sc = keep.tile([P, 3, 2 * H], U8, name="w_sc", align_bytes=64)
+        x_codes = keep.tile([P, B, 2, T], U32, name="x_codes", align_bytes=64)
+        x_sc = keep.tile([P, B, 2, T], U8, name="x_sc", align_bytes=64)
+        d_sum = keep.tile([P, HB, T], F32, name="d_sum")
+        n_sum = keep.tile([P, HB, T], F32, name="n_sum")
+        hw = keep.tile([P, J, H], F32, name="hw")
+        th = keep.tile([P, B, HB, T], F32, name="th")
+        b_rows = keep.tile([P, P], BF16, name="b_rows")
+        b_rows32 = keep.tile([P, P], F32, name="b_rows32")
+        b_cols = keep.tile([P, 8], F32, name="b_cols")
 
         w_dram = (Wk, Wv, Wq)
+        w_raw = {}
         x_tiles = {}
         grp_tiles = {}
+        e_tiles = {}
+        p_tiles = {}
 
-        def load_w(m, r):
-            nc.sync.dma_start(out=w_raw[:, 3 * m + r, :], in_=w_dram[m][r * P : (r + 1) * P, :])
+        def load_w(m):
+            w_raw[m] = stage.tile([P, HB, DM], BF16, name="w_raw", tag="six", bufs=4, align_bytes=64)
+            nc.sync.dma_start(out=w_raw[m][:], in_=w_dram[m].rearrange("(r p) k -> p r k", p=P))
 
-        def load_x(b, halves):
-            xr = stage.tile([P, J, DM], BF16, name="x_raw", tag="x_raw", bufs=XBUFS)
-            x_tiles[b] = xr
+        def load_x(b, parts):
+            x_tiles[b] = stage.tile([P, J, DM], BF16, name="x_raw", tag="x_raw", bufs=XBUFS)
             src = x[b].rearrange("(p j) k -> p j k", j=J)
-            if halves:
-                nc.sync.dma_start(out=xr[:, 0:2, :], in_=src[:, 0:2, :])
-            else:
-                nc.sync.dma_start(out=xr[:], in_=src)
-
-        def load_x_second_half(b):
-            src = x[b].rearrange("(p j) k -> p j k", j=J)
-            nc.sync.dma_start(out=x_tiles[b][:, 2:4, :], in_=src[:, 2:4, :])
+            step = J // parts
+            for i in range(parts):
+                nc.sync.dma_start(
+                    out=x_tiles[b][:, i * step : (i + 1) * step, :], in_=src[:, i * step : (i + 1) * step, :]
+                )
 
         def transpose_words(dst_bank, src_bf16):
             words = src_bf16.bitcast(F32)
@@ -81,43 +86,48 @@ def tile_aftattention_t_kernel(tc, x, Wq, bq, Wk, bk, Wv, bv, wbias, out):
                     dst_bank[:, c * P : (c + 1) * P], words[:, c * P : (c + 1) * P], ident[:]
                 )
 
-        w_grp32 = w_grp[:].bitcast(F32).rearrange("p (m g h u) -> p m g h u", m=3, g=2, u=2)
+        def t_w(m, engines):
+            grp = stage.tile([P, 2 * H * 4], BF16, name="w_grp", tag="six", bufs=4, align_bytes=64)
+            grp32 = grp[:].bitcast(F32).rearrange("p (g h u) -> p g h u", g=2, u=2)
+            for r in range(HB):
+                ps = bank()
+                transpose_words(ps, w_raw[m][:, r, :])
+                src = ps[:].rearrange("p (g u r) -> p g r u", g=2, u=2)
+                dst = grp32[:, :, r * P : (r + 1) * P, :]
+                if engines[r] == "s":
+                    nc.scalar.copy(out=dst, in_=src)
+                else:
+                    nc.vector.tensor_copy(out=dst, in_=src)
+            return grp
 
-        def t_w(m, r, tag, on_scalar):
-            bk_ = bank(tag)
-            transpose_words(bk_, w_raw[:, 3 * m + r, :])
-            src = bk_[:].rearrange("p (g u r) -> p g r u", g=2, u=2)
-            dst = w_grp32[:, m, :, r * P : (r + 1) * P, :]
-            if on_scalar:
-                nc.scalar.copy(out=dst, in_=src)
-            else:
-                nc.vector.tensor_copy(out=dst, in_=src)
-
-        def q_w(m, c0, c1):
-            for g in range(2):
-                off = ((m * 2 + g) * H + c0) * 4
+        def q_w(m, grp):
+            for c0, c1 in ((0, 512), (512, 768)):
                 nc.vector.quantize_mx(
-                    out=w_codes[:, m, g, c0:c1].bitcast(FP8X4),
-                    scales=w_sc[:, m, g, c0:c1],
-                    in_=w_grp[:, off : off + 4 * (c1 - c0)],
+                    out=w_codes[:, m, c0:c1].bitcast(FP8X4),
+                    scales=w_sc[:, m, c0:c1],
+                    in_=grp[:, 4 * c0 : 4 * c1],
                 )
 
         def t_x(q):
+            if q >= 2 * B:
+                return
             b, half = q // 2, q % 2
             grp = stage.tile([P, 2048], BF16, name="x_grp", tag="x_grp", bufs=3, align_bytes=64)
             grp_tiles[q] = grp
             grp32 = grp[:].bitcast(F32).rearrange("p (g r u) -> p g r u", g=2, u=2)
             for s in range(2):
-                bk_ = bank("tp")
-                transpose_words(bk_, x_tiles[b][:, 2 * half + s, :])
+                ps = bank()
+                transpose_words(ps, x_tiles[b][:, 2 * half + s, :])
                 nc.scalar.copy(
                     out=grp32[:, :, s * P : (s + 1) * P, :],
-                    in_=bk_[:].rearrange("p (g u r) -> p g r u", g=2, u=2),
+                    in_=ps[:].rearrange("p (g u r) -> p g r u", g=2, u=2),
                 )
             if half == 1 and b + XBUFS < B:
-                load_x(b + XBUFS, False)
+                load_x(b + XBUFS, 1)
 
         def q_x(q):
+            if q >= 2 * B:
+                return
             b, half = q // 2, q % 2
             grp = grp_tiles[q]
             for g in range(2):
@@ -127,129 +137,210 @@ def tile_aftattention_t_kernel(tc, x, Wq, bq, Wk, bk, Wv, bv, wbias, out):
                     in_=grp[:, g * 1024 : (g + 1) * 1024],
                 )
 
-        def project(dst_bank, b, j, m):
-            for c0, c1 in ((0, 256), (256, H)):
-                for g in range(2):
-                    nc.tensor.matmul_mx(
-                        out=dst_bank[:, c0:c1],
-                        lhsT=x_codes[:, b, g, j * P : (j + 1) * P].bitcast(FP8X4),
-                        lhsT_scale=x_sc[:, b, g, j * P : (j + 1) * P],
-                        rhs=w_codes[:, m, g, c0:c1].bitcast(FP8X4),
-                        rhs_scale=w_sc[:, m, g, c0:c1],
-                        start=(g == 0),
-                        stop=(g == 1),
-                    )
+        def project(m, b, hb):
+            ps = bank()
+            for g in range(2):
+                cols = slice(g * H + hb * P, g * H + (hb + 1) * P)
+                nc.tensor.matmul_mx(
+                    out=ps[:],
+                    lhsT=w_codes[:, m, cols].bitcast(FP8X4),
+                    lhsT_scale=w_sc[:, m, cols],
+                    rhs=x_codes[:, b, g, :].bitcast(FP8X4),
+                    rhs_scale=x_sc[:, b, g, :],
+                    start=(g == 0),
+                    stop=(g == 1),
+                )
+            return ps
 
-        def kv_pair(q, mid):
-            b, half = q // 2, q % 2
-            js = slice(2 * half, 2 * half + 2)
-            if b > 0:
-                e_t = stage.tile([P, 2, H], F32, name="e_t", tag="e_t", bufs=3)
-                p_t = stage.tile([P, 2, H], F32, name="p_t", tag="p_t", bufs=3)
-            for s in range(2):
-                j = 2 * half + s
-                kb = bank("kk")
-                project(kb, b, j, 0)
-                vb = bank("vv")
-                project(vb, b, j, 1)
-                e_dst = d_sum[:, j, :] if b == 0 else e_t[:, s, :]
-                p_dst = n_sum[:, j, :] if b == 0 else p_t[:, s, :]
-                nc.scalar.activation(out=e_dst, in_=kb[:, 0:H], func=ACT.Exp)
-                nc.vector.tensor_tensor(out=p_dst, in0=vb[:, 0:H], in1=e_dst, op=ALU.mult)
-                if s == 0 and mid:
-                    q_w(2, 256, H)
-            if b > 0:
-                nc.vector.tensor_tensor(out=n_sum[:, js, :], in0=n_sum[:, js, :], in1=p_t[:], op=ALU.add)
-                eng = nc.gpsimd if G_SUM_E else nc.vector
-                eng.tensor_tensor(out=d_sum[:, js, :], in0=d_sum[:, js, :], in1=e_t[:], op=ALU.add)
+        def k_unit(b, hb):
+            if not 0 <= b < B:
+                return
+            if hb == 0:
+                e_tiles[b] = stage.tile([P, HB, T], F32, name="e_t", tag="e_t", bufs=DV + 2)
+            ps = project(MK, b, hb)
+            nc.scalar.activation(out=e_tiles[b][:, hb, :], in_=ps[:], func=ACT.Exp)
 
-        for r in range(3):
-            load_w(0, r)
-        load_x(0, True)
-        for r in range(3):
-            load_w(1, r)
-        load_x_second_half(0)
-        load_x(1, True)
-        load_x_second_half(1)
-        load_x(2, False)
-        nc.sync.dma_start(out=w_raw[:, 6:9, :], in_=Wq.rearrange("(r p) k -> p r k", p=P))
-        load_x(3, False)
-        load_x(4, False)
-        nc.sync.dma_start(out=bq_b[:], in_=bq.partition_broadcast(P))
-        nc.sync.dma_start(out=bv_b[:], in_=bv.partition_broadcast(P))
+        def v_unit(b, hb):
+            if not 0 <= b < B:
+                return
+            if hb == 0 and b > 0:
+                p_tiles[b] = stage.tile([P, HB, T], F32, name="p_t", tag="six", bufs=4, align_bytes=64)
+            ps = project(MV, b, hb)
+            dst = n_sum[:, hb, :] if b == 0 else p_tiles[b][:, hb, :]
+            nc.vector.tensor_tensor(out=dst, in0=ps[:], in1=e_tiles[b][:, hb, :], op=ALU.mult)
 
-        for r in range(3):
-            t_w(0, r, "kk", r % 2 == 0)
-        t_x(0)
-        q_w(0, 0, 256)
-        q_w(0, 256, H)
-        for r in range(3):
-            t_w(1, r, "vv", r % 2 == 0)
-        t_x(1)
-        q_x(0)
-        q_w(1, 0, 256)
-        q_w(1, 256, H)
+        def q_unit(b, hb):
+            if not 0 <= b < B:
+                return
+            ps = project(MQ, b, hb)
+            nc.scalar.activation(
+                out=th[:, b, hb, :], in_=ps[:], func=ACT.Tanh, bias=b_cols[:, hb : hb + 1], scale=0.5
+            )
 
-        for q in range(NPAIR):
-            if q + LOOK < NPAIR:
-                t_x(q + LOOK)
-            elif q + LOOK == NPAIR:
-                t_w(2, 0, "tp", True)
-                t_w(2, 1, "tp", True)
-            else:
-                t_w(2, 2, "tp", True)
-            if q + 1 < NPAIR:
-                q_x(q + 1)
-            else:
-                q_w(2, 0, 256)
-            kv_pair(q, q == NPAIR - 1)
+        def sum_e(b):
+            if not 1 <= b < B:
+                return
+            first = e_tiles[0][:] if b == 1 else d_sum[:]
+            nc.vector.tensor_tensor(out=d_sum[:], in0=first, in1=e_tiles[b][:], op=ALU.add)
 
-        tags = ("kk", "vv", "kk", "vv", "kk", "vv", "tp", "tp")
-        zq_tiles = {}
+        def sum_p(b, hbs):
+            if not 1 <= b < B:
+                return
+            nc.vector.tensor_tensor(
+                out=n_sum[:, hbs, :], in0=n_sum[:, hbs, :], in1=p_tiles[b][:, hbs, :], op=ALU.add
+            )
+
         o_tiles = {}
+        tt_banks = {}
 
-        def q_front(t):
-            b, j = t // J, t % J
-            qb = bank(tags[t % 8])
-            project(qb, b, j, 2)
-            zq = stage.tile([P, H], F32, name="zq", tag="zq", bufs=ZL + 2)
-            zq_tiles[t] = zq
-            nc.vector.tensor_tensor(out=zq[:], in0=qb[:, 0:H], in1=bq_b[:], op=ALU.add)
+        def tt(b, hb):
+            ps = bank()
+            tt_banks[(b, hb)] = ps
+            for j in range(J):
+                nc.tensor.transpose(ps[:, j * P : (j + 1) * P], th[:, b, hb, j * P : (j + 1) * P], ident[:])
 
-        def q_back(t):
-            b, j = t // J, t % J
-            if j == 0:
-                o_tiles[b] = stage.tile([P, J, H], F32, name="o_sb", tag="o_sb", bufs=3)
-            o_sb = o_tiles[b]
-            sg = stage.tile([P, H], F32, name="sg", tag="sg", bufs=4)
-            nc.scalar.activation(out=sg[:], in_=zq_tiles[t][:], func=ACT.Sigmoid)
-            eng = nc.gpsimd if (G_P7_MOD and t % G_P7_MOD == 1) else nc.vector
-            eng.tensor_tensor(out=o_sb[:, j, :], in0=sg[:], in1=n_sum[:, j, :], op=ALU.mult)
+        def finish(b, hb):
+            if b not in o_tiles:
+                o_tiles[b] = stage.tile([P, J, H], F32, name="o_sb", tag="x_raw", bufs=XBUFS)
+            cols = slice(hb * P, (hb + 1) * P)
+            nc.vector.scalar_tensor_tensor(
+                out=o_tiles[b][:, :, cols],
+                in0=tt_banks[(b, hb)][:].rearrange("p (j h) -> p j h", j=J),
+                scalar=1.0,
+                in1=hw[:, :, cols],
+                op0=ALU.add,
+                op1=ALU.mult,
+            )
             dst = out[b].rearrange("(p j) h -> p j h", j=J)
             if b == B - 1:
-                if j % 2 == 1:
-                    nc.sync.dma_start(out=dst[:, j - 1 : j + 1, :], in_=o_sb[:, j - 1 : j + 1, :])
-            elif j == J - 1:
-                nc.sync.dma_start(out=dst, in_=o_sb[:])
+                nc.sync.dma_start(out=dst[:, :, cols], in_=o_tiles[b][:, :, cols])
+            elif hb == HB - 1:
+                nc.sync.dma_start(out=dst, in_=o_tiles[b][:])
 
-        for t in range(ZL):
-            q_front(t)
-        for hp in range(2):
-            js = slice(2 * hp, 2 * hp + 2)
-            nc.scalar.activation(out=r_d[:, js, :], in_=d_sum[:, js, :], func=ACT.Ln)
-        for hp in range(2):
-            js = slice(2 * hp, 2 * hp + 2)
-            nc.scalar.activation(out=r_d[:, js, :], in_=r_d[:, js, :], func=ACT.Exp, scale=-1.0)
-        for hp in range(2):
-            js = slice(2 * hp, 2 * hp + 2)
-            nc.vector.tensor_tensor(out=n_sum[:, js, :], in0=n_sum[:, js, :], in1=r_d[:, js, :], op=ALU.mult)
-            nc.vector.tensor_tensor(
-                out=n_sum[:, js, :],
-                in0=n_sum[:, js, :],
-                in1=bv_b[:].unsqueeze(1).to_broadcast([P, 2, H]),
-                op=ALU.add,
+        def recip(hb, stage_no):
+            if stage_no == 0:
+                nc.scalar.activation(out=d_sum[:, hb, :], in_=d_sum[:, hb, :], func=ACT.Ln)
+            else:
+                nc.scalar.activation(out=d_sum[:, hb, :], in_=d_sum[:, hb, :], func=ACT.Exp, scale=-1.0)
+
+        def weighted(hb):
+            nc.vector.tensor_tensor(out=n_sum[:, hb, :], in0=n_sum[:, hb, :], in1=d_sum[:, hb, :], op=ALU.mult)
+            nc.scalar.activation(
+                out=n_sum[:, hb, :],
+                in_=n_sum[:, hb, :],
+                func=ACT.Identity,
+                bias=b_cols[:, HB + hb : HB + hb + 1],
+                scale=0.5,
             )
-        for t in range(B * J):
-            q_back(t)
-            if t + ZL < B * J:
-                q_front(t + ZL)
+            ps = bank()
+            for j in range(J):
+                nc.tensor.transpose(ps[:, j * P : (j + 1) * P], n_sum[:, hb, j * P : (j + 1) * P], ident[:])
+            nc.scalar.copy(
+                out=hw[:, :, hb * P : (hb + 1) * P], in_=ps[:].rearrange("p (j h) -> p j h", j=J)
+            )
+
+        nc.vector.memset(b_rows[:], 0.0)
+        nc.scalar.dma_start(out=b_rows[0:HB, :], in_=bq.rearrange("(r c) -> r c", c=P))
+        nc.scalar.dma_start(out=b_rows[HB : 2 * HB, :], in_=bv.rearrange("(r c) -> r c", c=P))
+
+        load_w(MK)
+        load_x(0, 2)
+        load_w(MV)
+        load_x(1, 2)
+        load_x(2, 2)
+        load_w(MQ)
+        load_x(3, 1)
+
+        warm = keep.tile([P, 1], F32, name="warm")
+        nc.vector.memset(warm[:], 0.0)
+        nc.scalar.activation(out=warm[:], in_=warm[:], func=ACT.Exp)
+        nc.vector.tensor_copy(out=b_rows32[:], in_=b_rows[:])
+        ps_b = bank()
+        nc.tensor.transpose(ps_b[:, 0:P], b_rows32[:], ident[:])
+        nc.vector.tensor_scalar_mul(out=b_cols[:], in0=ps_b[:, 0:8], scalar1=0.5)
+
+        g_k = t_w(MK, "svs")
+        t_x(0)
+        q_w(MK, g_k)
+        t_x(1)
+        q_x(0)
+        q_x(1)
+        g_v = t_w(MV, "vsv")
+        q_w(MV, g_v)
+
+        q_list = [(b, hb) for b in range(B) for hb in range(HB)]
+        q_done = [0]
+
+        def q_some(n, limit_b):
+            for unused in range(n):
+                if q_done[0] < len(q_list) and q_list[q_done[0]][0] <= limit_b:
+                    q_unit(q_list[q_done[0]][0], q_list[q_done[0]][1])
+                    q_done[0] += 1
+
+        tx_done = [2]
+
+        def tx_next():
+            t_x(tx_done[0])
+            tx_done[0] += 1
+
+        qx_done = [2]
+
+        def qx_upto(n):
+            while qx_done[0] < min(n, 2 * B):
+                q_x(qx_done[0])
+                qx_done[0] += 1
+
+        NF = B - LASTK
+        for i in range(NF):
+            if i > 0:
+                tx_next()
+            for hb in range(HB):
+                k_unit(i, hb)
+            if i == 0:
+                tx_next()
+            if i == 1:
+                g_q = t_w(MQ, "sss")
+            sum_p(i - 1, slice(0, HB))
+            qx_upto(tx_done[0])
+            tx_next()
+            if i >= XTRA0:
+                tx_next()
+            sum_e(i)
+            for hb in range(HB):
+                v_unit(i, hb)
+            qx_upto(tx_done[0] - (1 if i >= XTRA0 else 0))
+            if i == 1:
+                q_w(MQ, g_q)
+            q_some(QP1[i], i)
+        while tx_done[0] < 2 * B:
+            tx_next()
+        sum_p(NF - 1, slice(0, HB))
+        qx_upto(2 * B)
+        for i in range(NF, B):
+            for hb in range(HB):
+                k_unit(i, hb)
+            sum_e(i)
+            q_some(QP2[i - NF], B)
+        for hb in range(HB):
+            recip(hb, 0)
+        for hb in range(HB):
+            recip(hb, 1)
+        for i in range(NF, B):
+            for hb in range(HB):
+                v_unit(i, hb)
+        q_some(QP3, B)
+        units = [(2 * bb + b, hb) for bb in range(B // 2) for hb in range(HB) for b in range(2)]
+        for n in range(PRE):
+            tt(units[n][0], units[n][1])
+        for hb in range(HB):
+            for i in range(NF, B):
+                sum_p(i, slice(hb, hb + 1))
+            weighted(hb)
+        for n in range(PRE, AHEAD):
+            tt(units[n][0], units[n][1])
+        for n in range(len(units)):
+            finish(units[n][0], units[n][1])
+            if n % QEVERY == 0:
+                q_some(3, B)
+            if n + AHEAD < len(units):
+                tt(units[n + AHEAD][0], units[n + AHEAD][1])

@@ -19,15 +19,15 @@ FLOPS = 2 * B * T * DM * 3 * H
 
 PIN = True
 LASTK = 3
-DV = LASTK - 1
-QP1 = (0, 1, 1, 1, 1)
+QP1 = (0, 0, 2, 1, 1)
 QP2 = (2, 2, 3)
-QP3 = 4
-PRE = 2
+QP3 = 2
+QW3 = (2, 1)
+PRE = 3
 QEVERY = 3
 XTRA0 = 1
+TWQ = 2
 AHEAD = 5
-OBUFS = 3
 XBUFS = 4
 MK, MV, MQ = 0, 1, 2
 
@@ -58,17 +58,22 @@ def tile_aftattention_t_kernel(tc, x, Wq, bq, Wk, bk, Wv, bv, wbias, out):
         b_rows = keep.tile([P, P], BF16, name="b_rows")
         b_rows32 = keep.tile([P, P], F32, name="b_rows32")
         b_cols = keep.tile([P, 8], F32, name="b_cols")
+        warm = keep.tile([P, 1], F32, name="warm")
 
         w_dram = (Wk, Wv, Wq)
         w_raw = {}
+        w_grp = {}
         x_tiles = {}
         grp_tiles = {}
         e_tiles = {}
         p_tiles = {}
+        o_tiles = {}
+        tt_banks = {}
 
-        def load_w(m):
-            w_raw[m] = stage.tile([P, HB, DM], BF16, name="w_raw", tag="six", bufs=4, align_bytes=64)
-            nc.sync.dma_start(out=w_raw[m][:], in_=w_dram[m].rearrange("(r p) k -> p r k", p=P))
+        def load_w(m, r):
+            if r == 0:
+                w_raw[m] = stage.tile([P, HB, DM], BF16, name="w_raw", tag="six", bufs=5, align_bytes=64)
+            nc.sync.dma_start(out=w_raw[m][:, r, :], in_=w_dram[m][r * P : (r + 1) * P, :])
 
         def load_x(b, parts):
             x_tiles[b] = stage.tile([P, J, DM], BF16, name="x_raw", tag="x_raw", bufs=XBUFS)
@@ -86,31 +91,29 @@ def tile_aftattention_t_kernel(tc, x, Wq, bq, Wk, bk, Wv, bv, wbias, out):
                     dst_bank[:, c * P : (c + 1) * P], words[:, c * P : (c + 1) * P], ident[:]
                 )
 
-        def t_w(m, engines):
-            grp = stage.tile([P, 2 * H * 4], BF16, name="w_grp", tag="six", bufs=4, align_bytes=64)
-            grp32 = grp[:].bitcast(F32).rearrange("p (g h u) -> p g h u", g=2, u=2)
-            for r in range(HB):
-                ps = bank()
-                transpose_words(ps, w_raw[m][:, r, :])
-                src = ps[:].rearrange("p (g u r) -> p g r u", g=2, u=2)
-                dst = grp32[:, :, r * P : (r + 1) * P, :]
-                if engines[r] == "s":
-                    nc.scalar.copy(out=dst, in_=src)
-                else:
-                    nc.vector.tensor_copy(out=dst, in_=src)
-            return grp
+        def t_w(m, r, engine):
+            if r == 0:
+                w_grp[m] = stage.tile([P, 2 * H * 4], BF16, name="w_grp", tag="six", bufs=5, align_bytes=64)
+            grp32 = w_grp[m][:].bitcast(F32).rearrange("p (g h u) -> p g h u", g=2, u=2)
+            ps = bank()
+            transpose_words(ps, w_raw[m][:, r, :])
+            src = ps[:].rearrange("p (g u r) -> p g r u", g=2, u=2)
+            dst = grp32[:, :, r * P : (r + 1) * P, :]
+            if engine == "s":
+                nc.scalar.copy(out=dst, in_=src)
+            else:
+                nc.vector.tensor_copy(out=dst, in_=src)
 
-        def q_w(m, grp):
-            for c0, c1 in ((0, 512), (512, 768)):
+        def q_w(m, r):
+            for g in range(2):
+                cols = slice(g * H + r * P, g * H + (r + 1) * P)
                 nc.vector.quantize_mx(
-                    out=w_codes[:, m, c0:c1].bitcast(FP8X4),
-                    scales=w_sc[:, m, c0:c1],
-                    in_=grp[:, 4 * c0 : 4 * c1],
+                    out=w_codes[:, m, cols].bitcast(FP8X4),
+                    scales=w_sc[:, m, cols],
+                    in_=w_grp[m][:, 4 * (g * H + r * P) : 4 * (g * H + (r + 1) * P)],
                 )
 
         def t_x(q):
-            if q >= 2 * B:
-                return
             b, half = q // 2, q % 2
             grp = stage.tile([P, 2048], BF16, name="x_grp", tag="x_grp", bufs=3, align_bytes=64)
             grp_tiles[q] = grp
@@ -126,8 +129,6 @@ def tile_aftattention_t_kernel(tc, x, Wq, bq, Wk, bk, Wv, bv, wbias, out):
                 load_x(b + XBUFS, 1)
 
         def q_x(q):
-            if q >= 2 * B:
-                return
             b, half = q // 2, q % 2
             grp = grp_tiles[q]
             for g in range(2):
@@ -153,45 +154,41 @@ def tile_aftattention_t_kernel(tc, x, Wq, bq, Wk, bk, Wv, bv, wbias, out):
             return ps
 
         def k_unit(b, hb):
-            if not 0 <= b < B:
-                return
             if hb == 0:
-                e_tiles[b] = stage.tile([P, HB, T], F32, name="e_t", tag="e_t", bufs=DV + 2)
+                e_tiles[b] = stage.tile([P, HB, T], F32, name="e_t", tag="e_t", bufs=LASTK + 1)
             ps = project(MK, b, hb)
             nc.scalar.activation(out=e_tiles[b][:, hb, :], in_=ps[:], func=ACT.Exp)
 
         def v_unit(b, hb):
-            if not 0 <= b < B:
-                return
             if hb == 0 and b > 0:
-                p_tiles[b] = stage.tile([P, HB, T], F32, name="p_t", tag="six", bufs=4, align_bytes=64)
+                p_tiles[b] = stage.tile([P, HB, T], F32, name="p_t", tag="six", bufs=5, align_bytes=64)
             ps = project(MV, b, hb)
             dst = n_sum[:, hb, :] if b == 0 else p_tiles[b][:, hb, :]
-            nc.vector.tensor_tensor(out=dst, in0=ps[:], in1=e_tiles[b][:, hb, :], op=ALU.mult)
+            nc.vector.scalar_tensor_tensor(
+                out=dst,
+                in0=ps[:],
+                scalar=b_cols[:, HB + hb : HB + hb + 1],
+                in1=e_tiles[b][:, hb, :],
+                op0=ALU.add,
+                op1=ALU.mult,
+            )
 
         def q_unit(b, hb):
-            if not 0 <= b < B:
-                return
             ps = project(MQ, b, hb)
             nc.scalar.activation(
                 out=th[:, b, hb, :], in_=ps[:], func=ACT.Tanh, bias=b_cols[:, hb : hb + 1], scale=0.5
             )
 
         def sum_e(b):
-            if not 1 <= b < B:
-                return
-            first = e_tiles[0][:] if b == 1 else d_sum[:]
-            nc.vector.tensor_tensor(out=d_sum[:], in0=first, in1=e_tiles[b][:], op=ALU.add)
+            if b >= 1:
+                first = e_tiles[0][:] if b == 1 else d_sum[:]
+                nc.vector.tensor_tensor(out=d_sum[:], in0=first, in1=e_tiles[b][:], op=ALU.add)
 
         def sum_p(b, hbs):
-            if not 1 <= b < B:
-                return
-            nc.vector.tensor_tensor(
-                out=n_sum[:, hbs, :], in0=n_sum[:, hbs, :], in1=p_tiles[b][:, hbs, :], op=ALU.add
-            )
-
-        o_tiles = {}
-        tt_banks = {}
+            if b >= 1:
+                nc.vector.tensor_tensor(
+                    out=n_sum[:, hbs, :], in0=n_sum[:, hbs, :], in1=p_tiles[b][:, hbs, :], op=ALU.add
+                )
 
         def tt(b, hb):
             ps = bank()
@@ -217,57 +214,6 @@ def tile_aftattention_t_kernel(tc, x, Wq, bq, Wk, bk, Wv, bv, wbias, out):
             elif hb == HB - 1:
                 nc.sync.dma_start(out=dst, in_=o_tiles[b][:])
 
-        def recip(hb, stage_no):
-            if stage_no == 0:
-                nc.scalar.activation(out=d_sum[:, hb, :], in_=d_sum[:, hb, :], func=ACT.Ln)
-            else:
-                nc.scalar.activation(out=d_sum[:, hb, :], in_=d_sum[:, hb, :], func=ACT.Exp, scale=-1.0)
-
-        def weighted(hb):
-            nc.vector.tensor_tensor(out=n_sum[:, hb, :], in0=n_sum[:, hb, :], in1=d_sum[:, hb, :], op=ALU.mult)
-            nc.scalar.activation(
-                out=n_sum[:, hb, :],
-                in_=n_sum[:, hb, :],
-                func=ACT.Identity,
-                bias=b_cols[:, HB + hb : HB + hb + 1],
-                scale=0.5,
-            )
-            ps = bank()
-            for j in range(J):
-                nc.tensor.transpose(ps[:, j * P : (j + 1) * P], n_sum[:, hb, j * P : (j + 1) * P], ident[:])
-            nc.scalar.copy(
-                out=hw[:, :, hb * P : (hb + 1) * P], in_=ps[:].rearrange("p (j h) -> p j h", j=J)
-            )
-
-        nc.vector.memset(b_rows[:], 0.0)
-        nc.scalar.dma_start(out=b_rows[0:HB, :], in_=bq.rearrange("(r c) -> r c", c=P))
-        nc.scalar.dma_start(out=b_rows[HB : 2 * HB, :], in_=bv.rearrange("(r c) -> r c", c=P))
-
-        load_w(MK)
-        load_x(0, 2)
-        load_w(MV)
-        load_x(1, 2)
-        load_x(2, 2)
-        load_w(MQ)
-        load_x(3, 1)
-
-        warm = keep.tile([P, 1], F32, name="warm")
-        nc.vector.memset(warm[:], 0.0)
-        nc.scalar.activation(out=warm[:], in_=warm[:], func=ACT.Exp)
-        nc.vector.tensor_copy(out=b_rows32[:], in_=b_rows[:])
-        ps_b = bank()
-        nc.tensor.transpose(ps_b[:, 0:P], b_rows32[:], ident[:])
-        nc.vector.tensor_scalar_mul(out=b_cols[:], in0=ps_b[:, 0:8], scalar1=0.5)
-
-        g_k = t_w(MK, "svs")
-        t_x(0)
-        q_w(MK, g_k)
-        t_x(1)
-        q_x(0)
-        q_x(1)
-        g_v = t_w(MV, "vsv")
-        q_w(MV, g_v)
-
         q_list = [(b, hb) for b in range(B) for hb in range(HB)]
         q_done = [0]
 
@@ -277,18 +223,61 @@ def tile_aftattention_t_kernel(tc, x, Wq, bq, Wk, bk, Wv, bv, wbias, out):
                     q_unit(q_list[q_done[0]][0], q_list[q_done[0]][1])
                     q_done[0] += 1
 
-        tx_done = [2]
+        def weighted(hb, nq):
+            nc.vector.tensor_tensor(out=n_sum[:, hb, :], in0=n_sum[:, hb, :], in1=d_sum[:, hb, :], op=ALU.mult)
+            q_some(nq[0], B)
+            ps = bank()
+            for j in range(J):
+                nc.tensor.transpose(ps[:, j * P : (j + 1) * P], n_sum[:, hb, j * P : (j + 1) * P], ident[:])
+            q_some(nq[1], B)
+            nc.scalar.mul(
+                out=hw[:, :, hb * P : (hb + 1) * P], in_=ps[:].rearrange("p (j h) -> p j h", j=J), mul=0.5
+            )
+
+        tx_done = [0]
 
         def tx_next():
-            t_x(tx_done[0])
-            tx_done[0] += 1
+            if tx_done[0] < 2 * B:
+                t_x(tx_done[0])
+                tx_done[0] += 1
 
-        qx_done = [2]
+        qx_done = [0]
 
         def qx_upto(n):
             while qx_done[0] < min(n, 2 * B):
                 q_x(qx_done[0])
                 qx_done[0] += 1
+
+        nc.vector.memset(b_rows[:], 0.0)
+        nc.scalar.dma_start(out=b_rows[0:HB, :], in_=bq.rearrange("(r c) -> r c", c=P))
+        nc.scalar.dma_start(out=b_rows[HB : 2 * HB, :], in_=bv.rearrange("(r c) -> r c", c=P))
+        nc.vector.memset(warm[:], 0.0)
+        nc.scalar.activation(out=warm[:], in_=warm[:], func=ACT.Exp)
+
+        load_x(0, 2)
+        for r in range(HB):
+            load_w(MK, r)
+        for r in range(HB):
+            load_w(MV, r)
+        load_x(1, 2)
+        load_x(2, 2)
+        load_x(3, 1)
+
+        tx_next()
+        tx_next()
+        for r in range(HB):
+            load_w(MQ, r)
+        qx_upto(1)
+        t_w(MK, 0, "v")
+        q_w(MK, 0)
+        qx_upto(2)
+        t_w(MK, 1, "v")
+        t_w(MK, 2, "s")
+        q_w(MK, 1)
+        q_w(MK, 2)
+        t_w(MV, 0, "s")
+        nc.vector.tensor_copy(out=b_rows32[:], in_=b_rows[:])
+        q_w(MV, 0)
 
         NF = B - LASTK
         for i in range(NF):
@@ -297,20 +286,32 @@ def tile_aftattention_t_kernel(tc, x, Wq, bq, Wk, bk, Wv, bv, wbias, out):
             for hb in range(HB):
                 k_unit(i, hb)
             if i == 0:
+                t_w(MV, 1, "v")
+                t_w(MV, 2, "s")
+                ps_b = bank()
+                nc.tensor.transpose(ps_b[:, 0:P], b_rows32[:], ident[:])
                 tx_next()
-            if i == 1:
-                g_q = t_w(MQ, "sss")
+                tx_next()
+                q_w(MV, 1)
+                q_w(MV, 2)
+                nc.vector.tensor_scalar_mul(out=b_cols[:, 0:HB], in0=ps_b[:, 0:HB], scalar1=0.5)
+                nc.vector.tensor_copy(out=b_cols[:, HB : 2 * HB], in_=ps_b[:, HB : 2 * HB])
+            if i == TWQ:
+                for r in range(HB):
+                    t_w(MQ, r, "s")
             sum_p(i - 1, slice(0, HB))
             qx_upto(tx_done[0])
-            tx_next()
+            if i > 0:
+                tx_next()
             if i >= XTRA0:
                 tx_next()
             sum_e(i)
             for hb in range(HB):
                 v_unit(i, hb)
             qx_upto(tx_done[0] - (1 if i >= XTRA0 else 0))
-            if i == 1:
-                q_w(MQ, g_q)
+            if i == TWQ:
+                for r in range(HB):
+                    q_w(MQ, r)
             q_some(QP1[i], i)
         while tx_done[0] < 2 * B:
             tx_next()
@@ -322,9 +323,9 @@ def tile_aftattention_t_kernel(tc, x, Wq, bq, Wk, bk, Wv, bv, wbias, out):
             sum_e(i)
             q_some(QP2[i - NF], B)
         for hb in range(HB):
-            recip(hb, 0)
+            nc.scalar.activation(out=d_sum[:, hb, :], in_=d_sum[:, hb, :], func=ACT.Ln)
         for hb in range(HB):
-            recip(hb, 1)
+            nc.scalar.activation(out=d_sum[:, hb, :], in_=d_sum[:, hb, :], func=ACT.Exp, scale=-1.0)
         for i in range(NF, B):
             for hb in range(HB):
                 v_unit(i, hb)
@@ -335,7 +336,7 @@ def tile_aftattention_t_kernel(tc, x, Wq, bq, Wk, bk, Wv, bv, wbias, out):
         for hb in range(HB):
             for i in range(NF, B):
                 sum_p(i, slice(hb, hb + 1))
-            weighted(hb)
+            weighted(hb, QW3)
         for n in range(PRE, AHEAD):
             tt(units[n][0], units[n][1])
         for n in range(len(units)):

@@ -17,7 +17,7 @@ J = T // P
 HB = H // P
 FLOPS = 2 * B * T * DM * 3 * H
 
-PIN = True
+PIN = False
 LASTK = 3
 QP1 = (0, 0, 2, 1, 1)
 QP2 = (2, 2, 3)

@@ -15,21 +15,23 @@ B, T, DM, H = 8, 512, 1024, 384
 P = 128
 J = T // P
 HB = H // P
+PAIRS = 2 * B
 FLOPS = 2 * B * T * DM * 3 * H
 
-PIN = False
-LASTK = 3
-QP1 = (0, 0, 2, 1, 1)
-QP2 = (2, 2, 3)
-QP3 = 2
-QW3 = (2, 1)
-PRE = 3
-QEVERY = 3
-XTRA0 = 1
-TWQ = 2
-AHEAD = 5
-XBUFS = 4
 MK, MV, MQ = 0, 1, 2
+
+K_FIRST = 3
+EARLY = B - K_FIRST
+
+Q_AFTER_EARLY = (0, 0, 0, 2, 2)
+Q_AFTER_LATE_K = (1, 2, 4)
+Q_AFTER_LATE_V = 2
+Q_IN_MEAN = (2, 1)
+
+TANH_AHEAD = 6
+TANH_BEFORE_MEAN = 3
+
+X_BUFS = 4
 
 
 def tile_aftattention_t_kernel(tc, x, Wq, bq, Wk, bk, Wv, bv, wbias, out):
@@ -38,8 +40,6 @@ def tile_aftattention_t_kernel(tc, x, Wq, bq, Wk, bk, Wv, bv, wbias, out):
         keep = ctx.enter_context(tc.tile_pool(name="keep", bufs=1))
         stage = ctx.enter_context(tc.tile_pool(name="stage", bufs=2))
         psum = ctx.enter_context(tc.psum_pool(name="psum", bufs=8))
-        if PIN:
-            ctx.enter_context(tc.manual_schedule())
 
         def bank():
             return psum.tile([P, 512], F32, name="ps", tag="ps", bufs=8)
@@ -65,18 +65,19 @@ def tile_aftattention_t_kernel(tc, x, Wq, bq, Wk, bk, Wv, bv, wbias, out):
         w_grp = {}
         x_tiles = {}
         grp_tiles = {}
+        quantised = []
         e_tiles = {}
         p_tiles = {}
         o_tiles = {}
-        tt_banks = {}
+        tanh_banks = {}
 
-        def load_w(m, r):
-            if r == 0:
-                w_raw[m] = stage.tile([P, HB, DM], BF16, name="w_raw", tag="six", bufs=5, align_bytes=64)
-            nc.sync.dma_start(out=w_raw[m][:, r, :], in_=w_dram[m][r * P : (r + 1) * P, :])
+        def load_w(m):
+            w_raw[m] = stage.tile([P, HB, DM], BF16, name="w_raw", tag="six", bufs=5, align_bytes=64)
+            for r in range(HB):
+                nc.sync.dma_start(out=w_raw[m][:, r, :], in_=w_dram[m][r * P : (r + 1) * P, :])
 
         def load_x(b, parts):
-            x_tiles[b] = stage.tile([P, J, DM], BF16, name="x_raw", tag="x_raw", bufs=XBUFS)
+            x_tiles[b] = stage.tile([P, J, DM], BF16, name="x_raw", tag="x_raw", bufs=X_BUFS)
             src = x[b].rearrange("(p j) k -> p j k", j=J)
             step = J // parts
             for i in range(parts):
@@ -91,20 +92,22 @@ def tile_aftattention_t_kernel(tc, x, Wq, bq, Wk, bk, Wv, bv, wbias, out):
                     dst_bank[:, c * P : (c + 1) * P], words[:, c * P : (c + 1) * P], ident[:]
                 )
 
-        def t_w(m, r, engine):
+        def grouped(ps):
+            return ps[:].rearrange("p (g u r) -> p g r u", g=2, u=2)
+
+        def transpose_w(m, r, engine):
             if r == 0:
                 w_grp[m] = stage.tile([P, 2 * H * 4], BF16, name="w_grp", tag="six", bufs=5, align_bytes=64)
             grp32 = w_grp[m][:].bitcast(F32).rearrange("p (g h u) -> p g h u", g=2, u=2)
             ps = bank()
             transpose_words(ps, w_raw[m][:, r, :])
-            src = ps[:].rearrange("p (g u r) -> p g r u", g=2, u=2)
             dst = grp32[:, :, r * P : (r + 1) * P, :]
             if engine == "s":
-                nc.scalar.copy(out=dst, in_=src)
+                nc.scalar.copy(out=dst, in_=grouped(ps))
             else:
-                nc.vector.tensor_copy(out=dst, in_=src)
+                nc.vector.tensor_copy(out=dst, in_=grouped(ps))
 
-        def q_w(m, r):
+        def quantise_w(m, r):
             for g in range(2):
                 cols = slice(g * H + r * P, g * H + (r + 1) * P)
                 nc.vector.quantize_mx(
@@ -113,30 +116,31 @@ def tile_aftattention_t_kernel(tc, x, Wq, bq, Wk, bk, Wv, bv, wbias, out):
                     in_=w_grp[m][:, 4 * (g * H + r * P) : 4 * (g * H + (r + 1) * P)],
                 )
 
-        def t_x(q):
-            b, half = q // 2, q % 2
-            grp = stage.tile([P, 2048], BF16, name="x_grp", tag="x_grp", bufs=3, align_bytes=64)
-            grp_tiles[q] = grp
-            grp32 = grp[:].bitcast(F32).rearrange("p (g r u) -> p g r u", g=2, u=2)
-            for s in range(2):
-                ps = bank()
-                transpose_words(ps, x_tiles[b][:, 2 * half + s, :])
-                nc.scalar.copy(
-                    out=grp32[:, :, s * P : (s + 1) * P, :],
-                    in_=ps[:].rearrange("p (g u r) -> p g r u", g=2, u=2),
-                )
-            if half == 1 and b + XBUFS < B:
-                load_x(b + XBUFS, 1)
+        def transpose_x_upto(n):
+            while len(grp_tiles) < n:
+                q = len(grp_tiles)
+                b, half = q // 2, q % 2
+                grp = stage.tile([P, 2048], BF16, name="x_grp", tag="x_grp", bufs=3, align_bytes=64)
+                grp_tiles[q] = grp
+                grp32 = grp[:].bitcast(F32).rearrange("p (g r u) -> p g r u", g=2, u=2)
+                for s in range(2):
+                    ps = bank()
+                    transpose_words(ps, x_tiles[b][:, 2 * half + s, :])
+                    nc.scalar.copy(out=grp32[:, :, s * P : (s + 1) * P, :], in_=grouped(ps))
+                if half == 1 and b + X_BUFS < B:
+                    load_x(b + X_BUFS, 1)
 
-        def q_x(q):
-            b, half = q // 2, q % 2
-            grp = grp_tiles[q]
-            for g in range(2):
-                nc.vector.quantize_mx(
-                    out=x_codes[:, b, g, half * 256 : (half + 1) * 256].bitcast(FP8X4),
-                    scales=x_sc[:, b, g, half * 256 : (half + 1) * 256],
-                    in_=grp[:, g * 1024 : (g + 1) * 1024],
-                )
+        def quantise_x_upto(n):
+            while len(quantised) < n:
+                q = len(quantised)
+                quantised.append(q)
+                b, half = q // 2, q % 2
+                for g in range(2):
+                    nc.vector.quantize_mx(
+                        out=x_codes[:, b, g, half * 256 : (half + 1) * 256].bitcast(FP8X4),
+                        scales=x_sc[:, b, g, half * 256 : (half + 1) * 256],
+                        in_=grp_tiles[q][:, g * 1024 : (g + 1) * 1024],
+                    )
 
         def project(m, b, hb):
             ps = bank()
@@ -153,56 +157,74 @@ def tile_aftattention_t_kernel(tc, x, Wq, bq, Wk, bk, Wv, bv, wbias, out):
                 )
             return ps
 
-        def k_unit(b, hb):
-            if hb == 0:
-                e_tiles[b] = stage.tile([P, HB, T], F32, name="e_t", tag="e_t", bufs=LASTK + 1)
-            ps = project(MK, b, hb)
-            nc.scalar.activation(out=e_tiles[b][:, hb, :], in_=ps[:], func=ACT.Exp)
+        def k_units(b):
+            e_tiles[b] = stage.tile([P, HB, T], F32, name="e_t", tag="e_t", bufs=K_FIRST + 1)
+            for hb in range(HB):
+                ps = project(MK, b, hb)
+                nc.scalar.activation(out=e_tiles[b][:, hb, :], in_=ps[:], func=ACT.Exp)
 
-        def v_unit(b, hb):
-            if hb == 0 and b > 0:
+        def v_units(b):
+            if b > 0:
                 p_tiles[b] = stage.tile([P, HB, T], F32, name="p_t", tag="six", bufs=5, align_bytes=64)
-            ps = project(MV, b, hb)
-            dst = n_sum[:, hb, :] if b == 0 else p_tiles[b][:, hb, :]
-            nc.vector.scalar_tensor_tensor(
-                out=dst,
-                in0=ps[:],
-                scalar=b_cols[:, HB + hb : HB + hb + 1],
-                in1=e_tiles[b][:, hb, :],
-                op0=ALU.add,
-                op1=ALU.mult,
-            )
+            for hb in range(HB):
+                ps = project(MV, b, hb)
+                nc.vector.scalar_tensor_tensor(
+                    out=n_sum[:, hb, :] if b == 0 else p_tiles[b][:, hb, :],
+                    in0=ps[:],
+                    scalar=b_cols[:, HB + hb : HB + hb + 1],
+                    in1=e_tiles[b][:, hb, :],
+                    op0=ALU.add,
+                    op1=ALU.mult,
+                )
 
-        def q_unit(b, hb):
-            ps = project(MQ, b, hb)
-            nc.scalar.activation(
-                out=th[:, b, hb, :], in_=ps[:], func=ACT.Tanh, bias=b_cols[:, hb : hb + 1], scale=0.5
-            )
+        q_order = [(b, hb) for b in range(B) for hb in range(HB)]
+        q_issued = []
 
-        def sum_e(b):
+        def q_units(n):
+            for b, hb in q_order[len(q_issued) : len(q_issued) + n]:
+                assert 2 * b + 2 <= len(quantised)
+                q_issued.append((b, hb))
+                ps = project(MQ, b, hb)
+                nc.scalar.activation(
+                    out=th[:, b, hb, :], in_=ps[:], func=ACT.Tanh, bias=b_cols[:, hb : hb + 1], scale=0.5
+                )
+
+        def add_exponentials(b):
             if b >= 1:
                 first = e_tiles[0][:] if b == 1 else d_sum[:]
                 nc.vector.tensor_tensor(out=d_sum[:], in0=first, in1=e_tiles[b][:], op=ALU.add)
 
-        def sum_p(b, hbs):
+        def add_products(b, hbs):
             if b >= 1:
                 nc.vector.tensor_tensor(
                     out=n_sum[:, hbs, :], in0=n_sum[:, hbs, :], in1=p_tiles[b][:, hbs, :], op=ALU.add
                 )
 
-        def tt(b, hb):
+        def tokens_to_partitions(src):
             ps = bank()
-            tt_banks[(b, hb)] = ps
             for j in range(J):
-                nc.tensor.transpose(ps[:, j * P : (j + 1) * P], th[:, b, hb, j * P : (j + 1) * P], ident[:])
+                nc.tensor.transpose(ps[:, j * P : (j + 1) * P], src[:, j * P : (j + 1) * P], ident[:])
+            return ps
+
+        def weighted_mean(hb):
+            nc.vector.tensor_tensor(out=n_sum[:, hb, :], in0=n_sum[:, hb, :], in1=d_sum[:, hb, :], op=ALU.mult)
+            q_units(Q_IN_MEAN[0])
+            ps = tokens_to_partitions(n_sum[:, hb, :])
+            q_units(Q_IN_MEAN[1])
+            nc.scalar.mul(
+                out=hw[:, :, hb * P : (hb + 1) * P], in_=ps[:].rearrange("p (j h) -> p j h", j=J), mul=0.5
+            )
+
+        def transpose_tanh(b, hb):
+            tanh_banks[(b, hb)] = tokens_to_partitions(th[:, b, hb, :])
 
         def finish(b, hb):
             if b not in o_tiles:
-                o_tiles[b] = stage.tile([P, J, H], F32, name="o_sb", tag="x_raw", bufs=XBUFS)
+                o_tiles[b] = stage.tile([P, J, H], F32, name="o_sb", tag="x_raw", bufs=X_BUFS)
             cols = slice(hb * P, (hb + 1) * P)
             nc.vector.scalar_tensor_tensor(
                 out=o_tiles[b][:, :, cols],
-                in0=tt_banks[(b, hb)][:].rearrange("p (j h) -> p j h", j=J),
+                in0=tanh_banks[(b, hb)][:].rearrange("p (j h) -> p j h", j=J),
                 scalar=1.0,
                 in1=hw[:, :, cols],
                 op0=ALU.add,
@@ -214,40 +236,6 @@ def tile_aftattention_t_kernel(tc, x, Wq, bq, Wk, bk, Wv, bv, wbias, out):
             elif hb == HB - 1:
                 nc.sync.dma_start(out=dst, in_=o_tiles[b][:])
 
-        q_list = [(b, hb) for b in range(B) for hb in range(HB)]
-        q_done = [0]
-
-        def q_some(n, limit_b):
-            for unused in range(n):
-                if q_done[0] < len(q_list) and q_list[q_done[0]][0] <= limit_b:
-                    q_unit(q_list[q_done[0]][0], q_list[q_done[0]][1])
-                    q_done[0] += 1
-
-        def weighted(hb, nq):
-            nc.vector.tensor_tensor(out=n_sum[:, hb, :], in0=n_sum[:, hb, :], in1=d_sum[:, hb, :], op=ALU.mult)
-            q_some(nq[0], B)
-            ps = bank()
-            for j in range(J):
-                nc.tensor.transpose(ps[:, j * P : (j + 1) * P], n_sum[:, hb, j * P : (j + 1) * P], ident[:])
-            q_some(nq[1], B)
-            nc.scalar.mul(
-                out=hw[:, :, hb * P : (hb + 1) * P], in_=ps[:].rearrange("p (j h) -> p j h", j=J), mul=0.5
-            )
-
-        tx_done = [0]
-
-        def tx_next():
-            if tx_done[0] < 2 * B:
-                t_x(tx_done[0])
-                tx_done[0] += 1
-
-        qx_done = [0]
-
-        def qx_upto(n):
-            while qx_done[0] < min(n, 2 * B):
-                q_x(qx_done[0])
-                qx_done[0] += 1
-
         nc.vector.memset(b_rows[:], 0.0)
         nc.scalar.dma_start(out=b_rows[0:HB, :], in_=bq.rearrange("(r c) -> r c", c=P))
         nc.scalar.dma_start(out=b_rows[HB : 2 * HB, :], in_=bv.rearrange("(r c) -> r c", c=P))
@@ -255,93 +243,82 @@ def tile_aftattention_t_kernel(tc, x, Wq, bq, Wk, bk, Wv, bv, wbias, out):
         nc.scalar.activation(out=warm[:], in_=warm[:], func=ACT.Exp)
 
         load_x(0, 2)
-        for r in range(HB):
-            load_w(MK, r)
-        for r in range(HB):
-            load_w(MV, r)
+        load_w(MK)
+        load_w(MV)
         load_x(1, 2)
         load_x(2, 2)
         load_x(3, 1)
 
-        tx_next()
-        tx_next()
-        for r in range(HB):
-            load_w(MQ, r)
-        qx_upto(1)
-        t_w(MK, 0, "v")
-        q_w(MK, 0)
-        qx_upto(2)
-        t_w(MK, 1, "v")
-        t_w(MK, 2, "s")
-        q_w(MK, 1)
-        q_w(MK, 2)
-        t_w(MV, 0, "s")
+        transpose_x_upto(2)
+        load_w(MQ)
+        quantise_x_upto(1)
+        transpose_w(MK, 0, "v")
+        quantise_w(MK, 0)
+        quantise_x_upto(2)
+        transpose_w(MK, 1, "v")
+        transpose_w(MK, 2, "s")
+        quantise_w(MK, 1)
+        quantise_w(MK, 2)
+        transpose_w(MV, 0, "s")
         nc.vector.tensor_copy(out=b_rows32[:], in_=b_rows[:])
-        q_w(MV, 0)
+        quantise_w(MV, 0)
+        k_units(0)
+        transpose_w(MV, 1, "v")
+        transpose_w(MV, 2, "s")
+        ps_b = bank()
+        nc.tensor.transpose(ps_b[:, 0:P], b_rows32[:], ident[:])
+        transpose_x_upto(4)
+        quantise_w(MV, 1)
+        quantise_w(MV, 2)
+        nc.vector.tensor_scalar_mul(out=b_cols[:, 0:HB], in0=ps_b[:, 0:HB], scalar1=0.5)
+        nc.vector.tensor_copy(out=b_cols[:, HB : 2 * HB], in_=ps_b[:, HB : 2 * HB])
+        quantise_x_upto(4)
+        v_units(0)
+        q_units(Q_AFTER_EARLY[0])
 
-        NF = B - LASTK
-        for i in range(NF):
-            if i > 0:
-                tx_next()
-            for hb in range(HB):
-                k_unit(i, hb)
-            if i == 0:
-                t_w(MV, 1, "v")
-                t_w(MV, 2, "s")
-                ps_b = bank()
-                nc.tensor.transpose(ps_b[:, 0:P], b_rows32[:], ident[:])
-                tx_next()
-                tx_next()
-                q_w(MV, 1)
-                q_w(MV, 2)
-                nc.vector.tensor_scalar_mul(out=b_cols[:, 0:HB], in0=ps_b[:, 0:HB], scalar1=0.5)
-                nc.vector.tensor_copy(out=b_cols[:, HB : 2 * HB], in_=ps_b[:, HB : 2 * HB])
-            if i == TWQ:
+        for b in range(1, EARLY):
+            transpose_x_upto(3 * b + 2)
+            k_units(b)
+            if b == 2:
                 for r in range(HB):
-                    t_w(MQ, r, "s")
-            sum_p(i - 1, slice(0, HB))
-            qx_upto(tx_done[0])
-            if i > 0:
-                tx_next()
-            if i >= XTRA0:
-                tx_next()
-            sum_e(i)
-            for hb in range(HB):
-                v_unit(i, hb)
-            qx_upto(tx_done[0] - (1 if i >= XTRA0 else 0))
-            if i == TWQ:
+                    transpose_w(MQ, r, "s")
+            add_products(b - 1, slice(0, HB))
+            quantise_x_upto(3 * b + 2)
+            transpose_x_upto(3 * b + 4)
+            add_exponentials(b)
+            v_units(b)
+            quantise_x_upto(3 * b + 3)
+            if b == 2:
                 for r in range(HB):
-                    q_w(MQ, r)
-            q_some(QP1[i], i)
-        while tx_done[0] < 2 * B:
-            tx_next()
-        sum_p(NF - 1, slice(0, HB))
-        qx_upto(2 * B)
-        for i in range(NF, B):
-            for hb in range(HB):
-                k_unit(i, hb)
-            sum_e(i)
-            q_some(QP2[i - NF], B)
+                    quantise_w(MQ, r)
+            q_units(Q_AFTER_EARLY[b])
+        add_products(EARLY - 1, slice(0, HB))
+        quantise_x_upto(PAIRS)
+
+        for b in range(EARLY, B):
+            k_units(b)
+            add_exponentials(b)
+            q_units(Q_AFTER_LATE_K[b - EARLY])
         for hb in range(HB):
             nc.scalar.activation(out=d_sum[:, hb, :], in_=d_sum[:, hb, :], func=ACT.Ln)
         for hb in range(HB):
             nc.scalar.activation(out=d_sum[:, hb, :], in_=d_sum[:, hb, :], func=ACT.Exp, scale=-1.0)
-        for i in range(NF, B):
-            for hb in range(HB):
-                v_unit(i, hb)
-        q_some(QP3, B)
-        units = [(2 * bb + b, hb) for bb in range(B // 2) for hb in range(HB) for b in range(2)]
-        for n in range(PRE):
-            tt(units[n][0], units[n][1])
+        for b in range(EARLY, B):
+            v_units(b)
+        q_units(Q_AFTER_LATE_V)
+
+        last = [(2 * bb + b, hb) for bb in range(B // 2) for hb in range(HB) for b in range(2)]
+        for b, hb in last[:TANH_BEFORE_MEAN]:
+            transpose_tanh(b, hb)
         for hb in range(HB):
-            for i in range(NF, B):
-                sum_p(i, slice(hb, hb + 1))
-            weighted(hb, QW3)
-        for n in range(PRE, AHEAD):
-            tt(units[n][0], units[n][1])
-        for n in range(len(units)):
-            finish(units[n][0], units[n][1])
-            if n % QEVERY == 0:
-                q_some(3, B)
-            if n + AHEAD < len(units):
-                tt(units[n + AHEAD][0], units[n + AHEAD][1])
+            for b in range(EARLY, B):
+                add_products(b, slice(hb, hb + 1))
+            weighted_mean(hb)
+        for b, hb in last[TANH_BEFORE_MEAN:TANH_AHEAD]:
+            transpose_tanh(b, hb)
+        for n in range(len(last)):
+            finish(last[n][0], last[n][1])
+            if n == 0:
+                q_units(len(q_order))
+            if n + TANH_AHEAD < len(last):
+                transpose_tanh(last[n + TANH_AHEAD][0], last[n + TANH_AHEAD][1])

from contextlib import ExitStack

import concourse.masks as masks
import concourse.mybir as mybir

F32 = mybir.dt.float32
BF16 = mybir.dt.bfloat16
U32 = mybir.dt.uint32
U8 = mybir.dt.uint8
FP8X4 = mybir.dt.float8_e4m3fn_x4
ACT = mybir.ActivationFunctionType
ALU = mybir.AluOpType

B, T, DM, H = 8, 512, 1024, 384
P = 128
J = T // P
HB = H // P
PAIRS = 2 * B
FLOPS = 2 * B * T * DM * 3 * H

MK, MV, MQ = 0, 1, 2

K_FIRST = 3
EARLY = B - K_FIRST

Q_AFTER_EARLY = (0, 0, 0, 2, 2)
Q_AFTER_LATE_K = (1, 2, 4)
Q_AFTER_LATE_V = 2
Q_IN_MEAN = (2, 1)

TANH_AHEAD = 6
TANH_BEFORE_MEAN = 3

X_BUFS = 4


def tile_aftattention_t_kernel(tc, x, Wq, bq, Wk, bk, Wv, bv, wbias, out):
    nc = tc.nc
    with ExitStack() as ctx:
        keep = ctx.enter_context(tc.tile_pool(name="keep", bufs=1))
        stage = ctx.enter_context(tc.tile_pool(name="stage", bufs=2))
        psum = ctx.enter_context(tc.psum_pool(name="psum", bufs=8))

        def bank():
            return psum.tile([P, 512], F32, name="ps", tag="ps", bufs=8)

        ident = keep.tile([P, P], F32, name="ident")
        masks.make_identity(nc, ident[:])

        w_codes = keep.tile([P, 3, 2 * H], U32, name="w_codes", align_bytes=64)
        w_sc = keep.tile([P, 3, 2 * H], U8, name="w_sc", align_bytes=64)
        x_codes = keep.tile([P, B, 2, T], U32, name="x_codes", align_bytes=64)
        x_sc = keep.tile([P, B, 2, T], U8, name="x_sc", align_bytes=64)
        d_sum = keep.tile([P, HB, T], F32, name="d_sum")
        n_sum = keep.tile([P, HB, T], F32, name="n_sum")
        hw = keep.tile([P, J, H], F32, name="hw")
        th = keep.tile([P, B, HB, T], F32, name="th")
        b_rows = keep.tile([P, P], BF16, name="b_rows")
        b_rows32 = keep.tile([P, P], F32, name="b_rows32")
        b_cols = keep.tile([P, 8], F32, name="b_cols")
        warm = keep.tile([P, 1], F32, name="warm")

        w_dram = (Wk, Wv, Wq)
        w_raw = {}
        w_grp = {}
        x_tiles = {}
        grp_tiles = {}
        quantised = []
        e_tiles = {}
        p_tiles = {}
        o_tiles = {}
        tanh_banks = {}

        def load_w(m):
            w_raw[m] = stage.tile([P, HB, DM], BF16, name="w_raw", tag="six", bufs=5, align_bytes=64)
            for r in range(HB):
                nc.sync.dma_start(out=w_raw[m][:, r, :], in_=w_dram[m][r * P : (r + 1) * P, :])

        def load_x(b, parts):
            x_tiles[b] = stage.tile([P, J, DM], BF16, name="x_raw", tag="x_raw", bufs=X_BUFS)
            src = x[b].rearrange("(p j) k -> p j k", j=J)
            step = J // parts
            for i in range(parts):
                nc.sync.dma_start(
                    out=x_tiles[b][:, i * step : (i + 1) * step, :], in_=src[:, i * step : (i + 1) * step, :]
                )

        def transpose_words(dst_bank, src_bf16):
            words = src_bf16.bitcast(F32)
            for c in range(4):
                nc.tensor.transpose(
                    dst_bank[:, c * P : (c + 1) * P], words[:, c * P : (c + 1) * P], ident[:]
                )

        def grouped(ps):
            return ps[:].rearrange("p (g u r) -> p g r u", g=2, u=2)

        def transpose_w(m, r, engine):
            if r == 0:
                w_grp[m] = stage.tile([P, 2 * H * 4], BF16, name="w_grp", tag="six", bufs=5, align_bytes=64)
            grp32 = w_grp[m][:].bitcast(F32).rearrange("p (g h u) -> p g h u", g=2, u=2)
            ps = bank()
            transpose_words(ps, w_raw[m][:, r, :])
            dst = grp32[:, :, r * P : (r + 1) * P, :]
            if engine == "s":
                nc.scalar.copy(out=dst, in_=grouped(ps))
            else:
                nc.vector.tensor_copy(out=dst, in_=grouped(ps))

        def quantise_w(m, r):
            for g in range(2):
                cols = slice(g * H + r * P, g * H + (r + 1) * P)
                nc.vector.quantize_mx(
                    out=w_codes[:, m, cols].bitcast(FP8X4),
                    scales=w_sc[:, m, cols],
                    in_=w_grp[m][:, 4 * (g * H + r * P) : 4 * (g * H + (r + 1) * P)],
                )

        def transpose_x_upto(n):
            while len(grp_tiles) < n:
                q = len(grp_tiles)
                b, half = q // 2, q % 2
                grp = stage.tile([P, 2048], BF16, name="x_grp", tag="x_grp", bufs=3, align_bytes=64)
                grp_tiles[q] = grp
                grp32 = grp[:].bitcast(F32).rearrange("p (g r u) -> p g r u", g=2, u=2)
                for s in range(2):
                    ps = bank()
                    transpose_words(ps, x_tiles[b][:, 2 * half + s, :])
                    nc.scalar.copy(out=grp32[:, :, s * P : (s + 1) * P, :], in_=grouped(ps))
                if half == 1 and b + X_BUFS < B:
                    load_x(b + X_BUFS, 1)

        def quantise_x_upto(n):
            while len(quantised) < n:
                q = len(quantised)
                quantised.append(q)
                b, half = q // 2, q % 2
                for g in range(2):
                    nc.vector.quantize_mx(
                        out=x_codes[:, b, g, half * 256 : (half + 1) * 256].bitcast(FP8X4),
                        scales=x_sc[:, b, g, half * 256 : (half + 1) * 256],
                        in_=grp_tiles[q][:, g * 1024 : (g + 1) * 1024],
                    )

        def project(m, b, hb):
            ps = bank()
            for g in range(2):
                cols = slice(g * H + hb * P, g * H + (hb + 1) * P)
                nc.tensor.matmul_mx(
                    out=ps[:],
                    lhsT=w_codes[:, m, cols].bitcast(FP8X4),
                    lhsT_scale=w_sc[:, m, cols],
                    rhs=x_codes[:, b, g, :].bitcast(FP8X4),
                    rhs_scale=x_sc[:, b, g, :],
                    start=(g == 0),
                    stop=(g == 1),
                )
            return ps

        def k_units(b):
            e_tiles[b] = stage.tile([P, HB, T], F32, name="e_t", tag="e_t", bufs=K_FIRST + 1)
            for hb in range(HB):
                ps = project(MK, b, hb)
                nc.scalar.activation(out=e_tiles[b][:, hb, :], in_=ps[:], func=ACT.Exp)

        def v_units(b):
            if b > 0:
                p_tiles[b] = stage.tile([P, HB, T], F32, name="p_t", tag="six", bufs=5, align_bytes=64)
            for hb in range(HB):
                ps = project(MV, b, hb)
                nc.vector.scalar_tensor_tensor(
                    out=n_sum[:, hb, :] if b == 0 else p_tiles[b][:, hb, :],
                    in0=ps[:],
                    scalar=b_cols[:, HB + hb : HB + hb + 1],
                    in1=e_tiles[b][:, hb, :],
                    op0=ALU.add,
                    op1=ALU.mult,
                )

        q_order = [(b, hb) for b in range(B) for hb in range(HB)]
        q_issued = []

        def q_units(n):
            for b, hb in q_order[len(q_issued) : len(q_issued) + n]:
                assert 2 * b + 2 <= len(quantised)
                q_issued.append((b, hb))
                ps = project(MQ, b, hb)
                nc.scalar.activation(
                    out=th[:, b, hb, :], in_=ps[:], func=ACT.Tanh, bias=b_cols[:, hb : hb + 1], scale=0.5
                )

        def add_exponentials(b):
            if b >= 1:
                first = e_tiles[0][:] if b == 1 else d_sum[:]
                nc.vector.tensor_tensor(out=d_sum[:], in0=first, in1=e_tiles[b][:], op=ALU.add)

        def add_products(b, hbs):
            if b >= 1:
                nc.vector.tensor_tensor(
                    out=n_sum[:, hbs, :], in0=n_sum[:, hbs, :], in1=p_tiles[b][:, hbs, :], op=ALU.add
                )

        def tokens_to_partitions(src):
            ps = bank()
            for j in range(J):
                nc.tensor.transpose(ps[:, j * P : (j + 1) * P], src[:, j * P : (j + 1) * P], ident[:])
            return ps

        def weighted_mean(hb):
            nc.vector.tensor_tensor(out=n_sum[:, hb, :], in0=n_sum[:, hb, :], in1=d_sum[:, hb, :], op=ALU.mult)
            q_units(Q_IN_MEAN[0])
            ps = tokens_to_partitions(n_sum[:, hb, :])
            q_units(Q_IN_MEAN[1])
            nc.scalar.mul(
                out=hw[:, :, hb * P : (hb + 1) * P], in_=ps[:].rearrange("p (j h) -> p j h", j=J), mul=0.5
            )

        def transpose_tanh(b, hb):
            tanh_banks[(b, hb)] = tokens_to_partitions(th[:, b, hb, :])

        def finish(b, hb):
            if b not in o_tiles:
                o_tiles[b] = stage.tile([P, J, H], F32, name="o_sb", tag="x_raw", bufs=X_BUFS)
            cols = slice(hb * P, (hb + 1) * P)
            nc.vector.scalar_tensor_tensor(
                out=o_tiles[b][:, :, cols],
                in0=tanh_banks[(b, hb)][:].rearrange("p (j h) -> p j h", j=J),
                scalar=1.0,
                in1=hw[:, :, cols],
                op0=ALU.add,
                op1=ALU.mult,
            )
            dst = out[b].rearrange("(p j) h -> p j h", j=J)
            if b == B - 1:
                nc.sync.dma_start(out=dst[:, :, cols], in_=o_tiles[b][:, :, cols])
            elif hb == HB - 1:
                nc.sync.dma_start(out=dst, in_=o_tiles[b][:])

        nc.vector.memset(b_rows[:], 0.0)
        nc.scalar.dma_start(out=b_rows[0:HB, :], in_=bq.rearrange("(r c) -> r c", c=P))
        nc.scalar.dma_start(out=b_rows[HB : 2 * HB, :], in_=bv.rearrange("(r c) -> r c", c=P))
        nc.vector.memset(warm[:], 0.0)
        nc.scalar.activation(out=warm[:], in_=warm[:], func=ACT.Exp)

        load_x(0, 2)
        load_w(MK)
        load_w(MV)
        load_x(1, 2)
        load_x(2, 2)
        load_x(3, 1)

        transpose_x_upto(2)
        load_w(MQ)
        quantise_x_upto(1)
        transpose_w(MK, 0, "v")
        quantise_w(MK, 0)
        quantise_x_upto(2)
        transpose_w(MK, 1, "v")
        transpose_w(MK, 2, "s")
        quantise_w(MK, 1)
        quantise_w(MK, 2)
        transpose_w(MV, 0, "s")
        nc.vector.tensor_copy(out=b_rows32[:], in_=b_rows[:])
        quantise_w(MV, 0)
        k_units(0)
        transpose_w(MV, 1, "v")
        transpose_w(MV, 2, "s")
        ps_b = bank()
        nc.tensor.transpose(ps_b[:, 0:P], b_rows32[:], ident[:])
        transpose_x_upto(4)
        quantise_w(MV, 1)
        quantise_w(MV, 2)
        nc.vector.tensor_scalar_mul(out=b_cols[:, 0:HB], in0=ps_b[:, 0:HB], scalar1=0.5)
        nc.vector.tensor_copy(out=b_cols[:, HB : 2 * HB], in_=ps_b[:, HB : 2 * HB])
        quantise_x_upto(4)
        v_units(0)
        q_units(Q_AFTER_EARLY[0])

        for b in range(1, EARLY):
            transpose_x_upto(3 * b + 2)
            k_units(b)
            if b == 2:
                for r in range(HB):
                    transpose_w(MQ, r, "s")
            add_products(b - 1, slice(0, HB))
            quantise_x_upto(3 * b + 2)
            transpose_x_upto(3 * b + 4)
            add_exponentials(b)
            v_units(b)
            quantise_x_upto(3 * b + 3)
            if b == 2:
                for r in range(HB):
                    quantise_w(MQ, r)
            q_units(Q_AFTER_EARLY[b])
        add_products(EARLY - 1, slice(0, HB))
        quantise_x_upto(PAIRS)

        for b in range(EARLY, B):
            k_units(b)
            add_exponentials(b)
            q_units(Q_AFTER_LATE_K[b - EARLY])
        for hb in range(HB):
            nc.scalar.activation(out=d_sum[:, hb, :], in_=d_sum[:, hb, :], func=ACT.Ln)
        for hb in range(HB):
            nc.scalar.activation(out=d_sum[:, hb, :], in_=d_sum[:, hb, :], func=ACT.Exp, scale=-1.0)
        for b in range(EARLY, B):
            v_units(b)
        q_units(Q_AFTER_LATE_V)

        last = [(2 * bb + b, hb) for bb in range(B // 2) for hb in range(HB) for b in range(2)]
        for b, hb in last[:TANH_BEFORE_MEAN]:
            transpose_tanh(b, hb)
        for hb in range(HB):
            for b in range(EARLY, B):
                add_products(b, slice(hb, hb + 1))
            weighted_mean(hb)
        for b, hb in last[TANH_BEFORE_MEAN:TANH_AHEAD]:
            transpose_tanh(b, hb)
        for n in range(len(last)):
            finish(last[n][0], last[n][1])
            if n == 0:
                q_units(len(q_order))
            if n + TANH_AHEAD < len(last):
                transpose_tanh(last[n + TANH_AHEAD][0], last[n + TANH_AHEAD][1])
